import numpy as np
import ml_dtypes


def mxq(x, axis, fmt="e4m3"):
    dtype, down = {"e4m3": (ml_dtypes.float8_e4m3fn, 7), "e5m2": (ml_dtypes.float8_e5m2, 14)}[fmt]
    v = np.moveaxis(np.asarray(x, np.float32).astype(ml_dtypes.bfloat16).astype(np.float64), axis, -1)
    blocks = v.reshape(v.shape[:-1] + (-1, 32))
    amax = np.abs(blocks).max(-1, keepdims=True)
    byte = np.maximum(np.where(amax > 0, np.frexp(amax)[1] - 1 + 127, 0) - down, 1)
    scale = np.exp2(byte - 127.0)
    codes = (blocks / scale).astype(np.float32).astype(dtype).astype(np.float64)
    return np.moveaxis((codes * scale).reshape(v.shape), -1, axis)


WIDE = False


def mx_kscale(k):
    if not WIDE:
        return np.ones(k)
    levels = np.array([20, -20, 10, -10, 0])
    a = np.random.permutation(np.resize(levels, k // 512 * 4)).reshape(k // 512, 4)
    idx = np.arange(k)
    return np.exp2(a[idx // 512, idx % 128 // 32])


BF16 = ml_dtypes.bfloat16


def bf(x):
    return np.asarray(x, np.float32).astype(BF16)


def f64(x):
    return np.asarray(x).astype(np.float64)


BATCH, IN_DIM, OUT_DIM = 4096, 512, 1024


def setup_inputs():
    u = mx_kscale(OUT_DIM)
    a = np.round(np.log2(u))
    x = np.random.standard_normal((BATCH, IN_DIM)) * (8.0 / np.sqrt(IN_DIM))
    shift = np.round(np.random.uniform(-10.0, -1.0, (IN_DIM, OUT_DIM))) - a[None, :]
    sign = np.round(np.random.uniform(0.0, 1.0, (IN_DIM, OUT_DIM)))
    bias = np.random.standard_normal((1, OUT_DIM)) * 0.5
    g = np.random.standard_normal((BATCH, OUT_DIM)) * np.exp2(np.random.randint(-12, 1, (BATCH, 1))) * u
    return {"x": bf(x), "shift": bf(shift), "sign": bf(sign), "bias": bf(bias), "grad_out": bf(g)}


def reference(x, shift, sign, bias, grad_out):
    W = np.exp2(f64(shift)) * np.power(-1.0, f64(sign))
    return mxq(f64(grad_out), 1, "e5m2") @ mxq(W, 1, "e4m3").T

@@ -1,0 +1,200 @@
+import math
+from contextlib import ExitStack
+
+import concourse.mybir as mybir
+from concourse.masks import make_identity
+
+F32 = mybir.dt.float32
+BF16 = mybir.dt.bfloat16
+U32 = mybir.dt.uint32
+U8 = mybir.dt.uint8
+E4M3X4 = mybir.dt.float8_e4m3fn_x4
+E5M2X4 = mybir.dt.float8_e5m2_x4
+ALU = mybir.AluOpType
+ACT = mybir.ActivationFunctionType
+
+P = 128
+TOKENS, IN_DIM, OUT_DIM = 4096, 512, 1024
+PASSES = OUT_DIM // 512
+WORDS = OUT_DIM // 2
+W_TILES = IN_DIM // P
+ROUNDS = (2, 2, 4, 4, 4, 4, 4, 4, 2, 2)
+LN2 = math.log(2.0)
+
+FLOPS = 2 * TOKENS * IN_DIM * OUT_DIM
+BYTES = 2 * IN_DIM * OUT_DIM * 2 + TOKENS * OUT_DIM * 2 + TOKENS * IN_DIM * 4
+
+
+def tile_denseshift_t_kernel(tc, x, shift, sign, bias, grad_out, out):
+    nc = tc.nc
+    assert sum(ROUNDS) * P == TOKENS
+    n_rounds = len(ROUNDS)
+    first_tile = [sum(ROUNDS[:r]) for r in range(n_rounds)]
+
+    with ExitStack() as ctx:
+        keep = ctx.enter_context(tc.tile_pool(name="keep", bufs=1))
+        ring = ctx.enter_context(tc.tile_pool(name="ring", bufs=3))
+        outs = ctx.enter_context(tc.tile_pool(name="outs", bufs=6))
+        psum = ctx.enter_context(tc.psum_pool(name="psum", bufs=4))
+        ctx.enter_context(tc.manual_schedule())
+
+        ident = keep.tile([P, P], F32, name="ident")
+        make_identity(nc, ident[:])
+        tiny = keep.tile([P, 2], F32, name="tiny")
+        nc.vector.memset(tiny[:, 0:1], 0.0)
+        nc.scalar.activation(out=tiny[:, 1:2], in_=tiny[:, 0:1], func=ACT.Exp)
+
+        shift_sb = keep.tile([P, W_TILES * OUT_DIM], BF16, name="shift_sb")
+        sign_sb = keep.tile([P, W_TILES * OUT_DIM], BF16, name="sign_sb")
+        for j in range(W_TILES):
+            cols = slice(j * OUT_DIM, (j + 1) * OUT_DIM)
+            rows = slice(j * P, (j + 1) * P)
+            nc.sync.dma_start(out=shift_sb[:, cols], in_=shift[rows, :])
+            nc.sync.dma_start(out=sign_sb[:, cols], in_=sign[rows, :])
+        g_raw = []
+        for r in range(n_rounds):
+            tiles = ROUNDS[r]
+            g_tile = keep.tile([P, tiles * OUT_DIM], BF16, name="g_raw%d" % r)
+            rows = slice(first_tile[r] * P, (first_tile[r] + tiles) * P)
+            nc.sync.dma_start(
+                out=g_tile[:].rearrange("p (j k) -> p j k", j=tiles),
+                in_=grad_out[rows, :].rearrange("(p j) k -> p j k", j=tiles),
+            )
+            g_raw.append(g_tile)
+
+        def transpose_row_tile(words):
+            bank = psum.tile([P, WORDS], F32, name="bank", tag="bank")
+            for q in range(WORDS // P):
+                nc.tensor.transpose(bank[:, q * P : (q + 1) * P], words[:, q * P : (q + 1) * P], ident[:])
+            return bank
+
+        def copy_on(engine_is_vector, dst, src):
+            if engine_is_vector:
+                nc.vector.tensor_copy(out=dst, in_=src)
+            else:
+                nc.scalar.copy(out=dst, in_=src)
+
+        def pairs_side_by_side(bank):
+            return bank[:].rearrange("p (g u r) -> p g r u", g=PASSES, u=2)
+
+        pow2 = keep.tile([P, W_TILES * OUT_DIM], BF16, name="pow2")
+        plus_minus = keep.tile([P, W_TILES * OUT_DIM], BF16, name="plus_minus")
+        w_sb = keep.tile([P, W_TILES * OUT_DIM], BF16, name="w_sb")
+        w_grouped = keep.tile([P, PASSES * IN_DIM * 4], BF16, name="w_grouped", align_bytes=64)
+        w_codes = keep.tile([P, PASSES * IN_DIM], U32, name="w_codes", align_bytes=64)
+        w_scales = keep.tile([P, PASSES * IN_DIM], U8, name="w_scales", align_bytes=64)
+        w_banks = {}
+
+        def w_exp(j):
+            cols = slice(j * OUT_DIM, (j + 1) * OUT_DIM)
+            nc.scalar.activation(out=pow2[:, cols], in_=shift_sb[:, cols], func=ACT.Exp, scale=LN2)
+
+        def w_plus_minus(j):
+            cols = slice(j * OUT_DIM, (j + 1) * OUT_DIM)
+            nc.vector.tensor_scalar(
+                out=plus_minus[:, cols], in0=sign_sb[:, cols], scalar1=-2.0, scalar2=1.0, op0=ALU.mult, op1=ALU.add
+            )
+
+        def w_mult(j):
+            cols = slice(j * OUT_DIM, (j + 1) * OUT_DIM)
+            nc.vector.tensor_tensor(out=w_sb[:, cols], in0=pow2[:, cols], in1=plus_minus[:, cols], op=ALU.mult)
+
+        def w_transpose(j):
+            w_banks[j] = transpose_row_tile(w_sb[:].bitcast(F32)[:, j * WORDS : (j + 1) * WORDS])
+
+        def w_copy(j, on_vector):
+            dst = w_grouped[:].bitcast(F32).rearrange("p (g n u) -> p g n u", g=PASSES, u=2)
+            copy_on(on_vector, dst[:, :, j * P : (j + 1) * P, :], pairs_side_by_side(w_banks[j]))
+
+        def w_quantise(j):
+            for g in range(PASSES):
+                words = slice(g * IN_DIM + j * P, g * IN_DIM + (j + 1) * P)
+                nc.vector.quantize_mx(
+                    out=w_codes[:, words].bitcast(E4M3X4),
+                    scales=w_scales[:, words],
+                    in_=w_grouped[:, 4 * (g * IN_DIM + j * P) : 4 * (g * IN_DIM + (j + 1) * P)],
+                )
+
+        state = {}
+
+        def g_transpose(r):
+            words = g_raw[r][:].bitcast(F32)
+            state[r] = {"banks": [transpose_row_tile(words[:, j * WORDS : (j + 1) * WORDS]) for j in range(ROUNDS[r])]}
+
+        def g_copy_quantise(r):
+            tiles = ROUNDS[r]
+            grouped = ring.tile([P, tiles * OUT_DIM], BF16, name="grouped", tag="grouped", align_bytes=64)
+            codes = ring.tile([P, tiles * OUT_DIM // 4], U32, name="codes", tag="codes", align_bytes=64)
+            scales = ring.tile([P, tiles * OUT_DIM // 4], U8, name="scales", tag="scales", align_bytes=64)
+            grouped_words = grouped[:].bitcast(F32)
+            for j in range(tiles):
+                dst = grouped_words[:, j * WORDS : (j + 1) * WORDS].rearrange("p (g r u) -> p g r u", g=PASSES, u=2)
+                copy_on(j % 2 == 1, dst, pairs_side_by_side(state[r]["banks"][j]))
+            for h in range(tiles // 2):
+                nc.vector.quantize_mx(
+                    out=codes[:, h * 512 : (h + 1) * 512].bitcast(E5M2X4),
+                    scales=scales[:, h * 512 : (h + 1) * 512],
+                    in_=grouped[:, h * 2048 : (h + 1) * 2048],
+                )
+            state[r]["codes"] = codes
+            state[r]["scales"] = scales
+
+        def g_multiply_store(r):
+            tiles = ROUNDS[r]
+            codes = state[r]["codes"]
+            scales = state[r]["scales"]
+            accs = []
+            for j in range(tiles):
+                acc = psum.tile([P, IN_DIM], F32, name="acc", tag="acc")
+                for g in range(PASSES):
+                    words = slice((j * PASSES + g) * P, (j * PASSES + g + 1) * P)
+                    nc.tensor.matmul_mx(
+                        out=acc[:],
+                        lhsT=codes[:, words].bitcast(E5M2X4),
+                        lhsT_scale=scales[:, words],
+                        rhs=w_codes[:, g * IN_DIM : (g + 1) * IN_DIM].bitcast(E4M3X4),
+                        rhs_scale=w_scales[:, g * IN_DIM : (g + 1) * IN_DIM],
+                        start=(g == 0),
+                        stop=(g == PASSES - 1),
+                    )
+                accs.append(acc)
+            result = outs.tile([P, tiles * IN_DIM], F32, name="result", tag="result")
+            for j in range(tiles):
+                copy_on((first_tile[r] + j) % 4 == 3, result[:, j * IN_DIM : (j + 1) * IN_DIM], accs[j][:])
+            rows = slice(first_tile[r] * P, (first_tile[r] + tiles) * P)
+            nc.sync.dma_start(
+                out=out[rows, :].rearrange("(p j) n -> p j n", j=tiles),
+                in_=result[:].rearrange("p (j n) -> p j n", j=tiles),
+            )
+
+        w_exp(0)
+        w_plus_minus(0)
+        w_mult(0)
+        w_transpose(0)
+        w_exp(1)
+        w_plus_minus(1)
+        w_mult(1)
+        w_transpose(1)
+        w_exp(2)
+        w_plus_minus(2)
+        w_copy(0, True)
+        w_mult(2)
+        w_transpose(2)
+        w_exp(3)
+        w_plus_minus(3)
+        w_quantise(0)
+        w_mult(3)
+        w_transpose(3)
+        w_copy(1, False)
+        w_quantise(1)
+        w_copy(2, False)
+        w_quantise(2)
+        g_transpose(0)
+        w_copy(3, False)
+        w_quantise(3)
+        g_copy_quantise(0)
+        for r in range(n_rounds):
+            if r + 1 < n_rounds:
+                g_transpose(r + 1)
+                g_copy_quantise(r + 1)
+            g_multiply_store(r)

@@ -18,8 +18,12 @@ TOKENS, IN_DIM, OUT_DIM = 4096, 512, 1024
 PASSES = OUT_DIM // 512
 WORDS = OUT_DIM // 2
 W_TILES = IN_DIM // P
-ROUNDS = (2, 2, 4, 4, 4, 4, 4, 4, 2, 2)
+J = 4
+ROUNDS = TOKENS // (J * P)
 LN2 = math.log(2.0)
+LOAD_PIECES = {0: ((0, 1), (1, 1), (2, 2)), 1: ((0, 2), (2, 2))}
+STORE_PIECES = {4: ((0, 2), (2, 2)), 5: ((0, 2), (2, 2)), 6: ((0, 2), (2, 2)), 7: ((0, 2), (2, 1), (3, 1))}
+DUMMIES = 0
 
 FLOPS = 2 * TOKENS * IN_DIM * OUT_DIM
 BYTES = 2 * IN_DIM * OUT_DIM * 2 + TOKENS * OUT_DIM * 2 + TOKENS * IN_DIM * 4
@@ -27,15 +31,12 @@ BYTES = 2 * IN_DIM * OUT_DIM * 2 + TOKENS * OUT_DIM * 2 + TOKENS * IN_DIM * 4
 
 def tile_denseshift_t_kernel(tc, x, shift, sign, bias, grad_out, out):
     nc = tc.nc
-    assert sum(ROUNDS) * P == TOKENS
-    n_rounds = len(ROUNDS)
-    first_tile = [sum(ROUNDS[:r]) for r in range(n_rounds)]
 
     with ExitStack() as ctx:
         keep = ctx.enter_context(tc.tile_pool(name="keep", bufs=1))
         ring = ctx.enter_context(tc.tile_pool(name="ring", bufs=3))
         outs = ctx.enter_context(tc.tile_pool(name="outs", bufs=6))
-        psum = ctx.enter_context(tc.psum_pool(name="psum", bufs=4))
+        psum = ctx.enter_context(tc.psum_pool(name="psum", bufs=1))
         ctx.enter_context(tc.manual_schedule())
 
         ident = keep.tile([P, P], F32, name="ident")
@@ -52,24 +53,28 @@ def tile_denseshift_t_kernel(tc, x, shift, sign, bias, grad_out, out):
             nc.sync.dma_start(out=shift_sb[:, cols], in_=shift[rows, :])
             nc.sync.dma_start(out=sign_sb[:, cols], in_=sign[rows, :])
         g_raw = []
-        for r in range(n_rounds):
-            tiles = ROUNDS[r]
-            g_tile = keep.tile([P, tiles * OUT_DIM], BF16, name="g_raw%d" % r)
-            rows = slice(first_tile[r] * P, (first_tile[r] + tiles) * P)
-            nc.sync.dma_start(
-                out=g_tile[:].rearrange("p (j k) -> p j k", j=tiles),
-                in_=grad_out[rows, :].rearrange("(p j) k -> p j k", j=tiles),
-            )
+        for r in range(ROUNDS):
+            g_tile = keep.tile([P, J * OUT_DIM], BF16, name="g_raw%d" % r)
+            src = grad_out[r * J * P : (r + 1) * J * P, :].rearrange("(p j) k -> p j k", j=J)
+            dst = g_tile[:].rearrange("p (j k) -> p j k", j=J)
+            for j0, nj in LOAD_PIECES.get(r, ((0, J),)):
+                nc.sync.dma_start(out=dst[:, j0 : j0 + nj, :], in_=src[:, j0 : j0 + nj, :])
             g_raw.append(g_tile)
 
+        taken = []
+
+        def next_bank():
+            taken.append(1)
+            return psum.tile([P, 512], F32, name="bank", tag="bank%d" % ((len(taken) - 1) % 8))
+
         def transpose_row_tile(words):
-            bank = psum.tile([P, WORDS], F32, name="bank", tag="bank")
+            bank = next_bank()
             for q in range(WORDS // P):
                 nc.tensor.transpose(bank[:, q * P : (q + 1) * P], words[:, q * P : (q + 1) * P], ident[:])
             return bank
 
-        def copy_on(engine_is_vector, dst, src):
-            if engine_is_vector:
+        def copy_on(engine, dst, src):
+            if engine == "v":
                 nc.vector.tensor_copy(out=dst, in_=src)
             else:
                 nc.scalar.copy(out=dst, in_=src)
@@ -102,9 +107,9 @@ def tile_denseshift_t_kernel(tc, x, shift, sign, bias, grad_out, out):
         def w_transpose(j):
             w_banks[j] = transpose_row_tile(w_sb[:].bitcast(F32)[:, j * WORDS : (j + 1) * WORDS])
 
-        def w_copy(j, on_vector):
+        def w_copy(j, engine):
             dst = w_grouped[:].bitcast(F32).rearrange("p (g n u) -> p g n u", g=PASSES, u=2)
-            copy_on(on_vector, dst[:, :, j * P : (j + 1) * P, :], pairs_side_by_side(w_banks[j]))
+            copy_on(engine, dst[:, :, j * P : (j + 1) * P, :], pairs_side_by_side(w_banks[j]))
 
         def w_quantise(j):
             for g in range(PASSES):
@@ -115,57 +120,64 @@ def tile_denseshift_t_kernel(tc, x, shift, sign, bias, grad_out, out):
                     in_=w_grouped[:, 4 * (g * IN_DIM + j * P) : 4 * (g * IN_DIM + (j + 1) * P)],
                 )
 
-        state = {}
+        banks = {}
+        grouped = {}
+        codes = {}
+        scales = {}
+        accs = {}
+        results = {}
 
-        def g_transpose(r):
+        def g_transpose(r, j0, nj):
             words = g_raw[r][:].bitcast(F32)
-            state[r] = {"banks": [transpose_row_tile(words[:, j * WORDS : (j + 1) * WORDS]) for j in range(ROUNDS[r])]}
+            for j in range(j0, j0 + nj):
+                banks[(r, j)] = transpose_row_tile(words[:, j * WORDS : (j + 1) * WORDS])
 
-        def g_copy_quantise(r):
-            tiles = ROUNDS[r]
-            grouped = ring.tile([P, tiles * OUT_DIM], BF16, name="grouped", tag="grouped", align_bytes=64)
-            codes = ring.tile([P, tiles * OUT_DIM // 4], U32, name="codes", tag="codes", align_bytes=64)
-            scales = ring.tile([P, tiles * OUT_DIM // 4], U8, name="scales", tag="scales", align_bytes=64)
-            grouped_words = grouped[:].bitcast(F32)
-            for j in range(tiles):
-                dst = grouped_words[:, j * WORDS : (j + 1) * WORDS].rearrange("p (g r u) -> p g r u", g=PASSES, u=2)
-                copy_on(j % 2 == 1, dst, pairs_side_by_side(state[r]["banks"][j]))
-            for h in range(tiles // 2):
-                nc.vector.quantize_mx(
-                    out=codes[:, h * 512 : (h + 1) * 512].bitcast(E5M2X4),
-                    scales=scales[:, h * 512 : (h + 1) * 512],
-                    in_=grouped[:, h * 2048 : (h + 1) * 2048],
-                )
-            state[r]["codes"] = codes
-            state[r]["scales"] = scales
+        def g_copy(r, j, engine):
+            if r not in grouped:
+                grouped[r] = ring.tile([P, J * OUT_DIM], BF16, name="grouped", tag="grouped", align_bytes=64)
+                codes[r] = ring.tile([P, J * OUT_DIM // 4], U32, name="codes", tag="codes", align_bytes=64)
+                scales[r] = ring.tile([P, J * OUT_DIM // 4], U8, name="scales", tag="scales", align_bytes=64)
+            dst = grouped[r][:].bitcast(F32)[:, j * WORDS : (j + 1) * WORDS]
+            copy_on(engine, dst.rearrange("p (g r u) -> p g r u", g=PASSES, u=2), pairs_side_by_side(banks[(r, j)]))
 
-        def g_multiply_store(r):
-            tiles = ROUNDS[r]
-            codes = state[r]["codes"]
-            scales = state[r]["scales"]
-            accs = []
-            for j in range(tiles):
-                acc = psum.tile([P, IN_DIM], F32, name="acc", tag="acc")
+        def g_quantise(r, j0, nj):
+            nc.vector.quantize_mx(
+                out=codes[r][:, j0 * 256 : (j0 + nj) * 256].bitcast(E5M2X4),
+                scales=scales[r][:, j0 * 256 : (j0 + nj) * 256],
+                in_=grouped[r][:, j0 * OUT_DIM : (j0 + nj) * OUT_DIM],
+            )
+
+        def g_multiply(r):
+            for j in range(J):
+                acc = next_bank()
                 for g in range(PASSES):
                     words = slice((j * PASSES + g) * P, (j * PASSES + g + 1) * P)
                     nc.tensor.matmul_mx(
                         out=acc[:],
-                        lhsT=codes[:, words].bitcast(E5M2X4),
-                        lhsT_scale=scales[:, words],
+                        lhsT=codes[r][:, words].bitcast(E5M2X4),
+                        lhsT_scale=scales[r][:, words],
                         rhs=w_codes[:, g * IN_DIM : (g + 1) * IN_DIM].bitcast(E4M3X4),
                         rhs_scale=w_scales[:, g * IN_DIM : (g + 1) * IN_DIM],
                         start=(g == 0),
                         stop=(g == PASSES - 1),
                     )
-                accs.append(acc)
-            result = outs.tile([P, tiles * IN_DIM], F32, name="result", tag="result")
-            for j in range(tiles):
-                copy_on((first_tile[r] + j) % 4 == 3, result[:, j * IN_DIM : (j + 1) * IN_DIM], accs[j][:])
-            rows = slice(first_tile[r] * P, (first_tile[r] + tiles) * P)
-            nc.sync.dma_start(
-                out=out[rows, :].rearrange("(p j) n -> p j n", j=tiles),
-                in_=result[:].rearrange("p (j n) -> p j n", j=tiles),
-            )
+                accs[(r, j)] = acc
+
+        def g_store(r):
+            result = outs.tile([P, J * IN_DIM], F32, name="result", tag="result")
+            for j in range(J):
+                copy_on("v" if j == J - 1 else "s", result[:, j * IN_DIM : (j + 1) * IN_DIM], accs[(r, j)][:])
+            dst = out[r * J * P : (r + 1) * J * P, :].rearrange("(p j) n -> p j n", j=J)
+            src = result[:].rearrange("p (j n) -> p j n", j=J)
+            for j0, nj in STORE_PIECES.get(r, ((0, J),)):
+                nc.sync.dma_start(out=dst[:, j0 : j0 + nj, :], in_=src[:, j0 : j0 + nj, :])
+
+        def g_prepare(r):
+            g_transpose(r, 0, J)
+            for j in range(J):
+                g_copy(r, j, "sv"[j % 2])
+            g_quantise(r, 0, 2)
+            g_quantise(r, 2, 2)
 
         w_exp(0)
         w_plus_minus(0)
@@ -177,24 +189,30 @@ def tile_denseshift_t_kernel(tc, x, shift, sign, bias, grad_out, out):
         w_transpose(1)
         w_exp(2)
         w_plus_minus(2)
-        w_copy(0, True)
         w_mult(2)
         w_transpose(2)
         w_exp(3)
         w_plus_minus(3)
-        w_quantise(0)
+        g_transpose(0, 0, 1)
         w_mult(3)
         w_transpose(3)
-        w_copy(1, False)
+        w_copy(0, "s")
+        w_quantise(0)
+        g_copy(0, 0, "v")
+        w_copy(1, "s")
         w_quantise(1)
-        w_copy(2, False)
+        g_transpose(0, 1, 3)
+        w_copy(2, "s")
         w_quantise(2)
-        g_transpose(0)
-        w_copy(3, False)
+        g_copy(0, 1, "v")
+        g_quantise(0, 0, 2)
+        w_copy(3, "s")
         w_quantise(3)
-        g_copy_quantise(0)
-        for r in range(n_rounds):
-            if r + 1 < n_rounds:
-                g_transpose(r + 1)
-                g_copy_quantise(r + 1)
-            g_multiply_store(r)
+        g_copy(0, 2, "s")
+        g_copy(0, 3, "v")
+        g_quantise(0, 2, 2)
+        for r in range(ROUNDS):
+            if r + 1 < ROUNDS:
+                g_prepare(r + 1)
+            g_multiply(r)
+            g_store(r)

@@ -20,9 +20,11 @@ WORDS = OUT_DIM // 2
 W_TILES = IN_DIM // P
 J = 4
 ROUNDS = TOKENS // (J * P)
+GJ = 2 * J
+GROUPS = ROUNDS // 2
 LN2 = math.log(2.0)
-LOAD_PIECES = {0: ((0, 1), (1, 1), (2, 2)), 1: ((0, 2), (2, 2))}
-STORE_PIECES = {4: ((0, 2), (2, 2)), 5: ((0, 2), (2, 2)), 6: ((0, 2), (2, 2)), 7: ((0, 2), (2, 1), (3, 1))}
+LOAD_PIECES = {0: ((0, 1), (1, 1), (2, 2), (4, 2), (6, 2)), 1: ((0, 4), (4, 4))}
+STORE_PIECES = {1: ((0, 8),), 3: ((0, 8),), 4: ((0, 4),), 5: ((4, 2), (6, 2)), 6: ((0, 1), (1, 1), (2, 1), (3, 1)), 7: ((4, 1), (5, 1), (6, 1), (7, 1))}
 DUMMIES = 0
 
 FLOPS = 2 * TOKENS * IN_DIM * OUT_DIM
@@ -35,7 +37,7 @@ def tile_denseshift_t_kernel(tc, x, shift, sign, bias, grad_out, out):
     with ExitStack() as ctx:
         keep = ctx.enter_context(tc.tile_pool(name="keep", bufs=1))
         ring = ctx.enter_context(tc.tile_pool(name="ring", bufs=3))
-        outs = ctx.enter_context(tc.tile_pool(name="outs", bufs=6))
+        outs = ctx.enter_context(tc.tile_pool(name="outs", bufs=4))
         psum = ctx.enter_context(tc.psum_pool(name="psum", bufs=1))
         ctx.enter_context(tc.manual_schedule())
 
@@ -53,11 +55,11 @@ def tile_denseshift_t_kernel(tc, x, shift, sign, bias, grad_out, out):
             nc.sync.dma_start(out=shift_sb[:, cols], in_=shift[rows, :])
             nc.sync.dma_start(out=sign_sb[:, cols], in_=sign[rows, :])
         g_raw = []
-        for r in range(ROUNDS):
-            g_tile = keep.tile([P, J * OUT_DIM], BF16, name="g_raw%d" % r)
-            src = grad_out[r * J * P : (r + 1) * J * P, :].rearrange("(p j) k -> p j k", j=J)
-            dst = g_tile[:].rearrange("p (j k) -> p j k", j=J)
-            for j0, nj in LOAD_PIECES.get(r, ((0, J),)):
+        for m in range(GROUPS):
+            g_tile = keep.tile([P, GJ * OUT_DIM], BF16, name="g_raw%d" % m)
+            src = grad_out[m * GJ * P : (m + 1) * GJ * P, :].rearrange("(p j) k -> p j k", j=GJ)
+            dst = g_tile[:].rearrange("p (j k) -> p j k", j=GJ)
+            for j0, nj in LOAD_PIECES.get(m, ((0, GJ),)):
                 nc.sync.dma_start(out=dst[:, j0 : j0 + nj, :], in_=src[:, j0 : j0 + nj, :])
             g_raw.append(g_tile)
 
@@ -128,9 +130,10 @@ def tile_denseshift_t_kernel(tc, x, shift, sign, bias, grad_out, out):
         results = {}
 
         def g_transpose(r, j0, nj):
-            words = g_raw[r][:].bitcast(F32)
+            words = g_raw[r // 2][:].bitcast(F32)
             for j in range(j0, j0 + nj):
-                banks[(r, j)] = transpose_row_tile(words[:, j * WORDS : (j + 1) * WORDS])
+                jj = (r % 2) * J + j
+                banks[(r, j)] = transpose_row_tile(words[:, jj * WORDS : (jj + 1) * WORDS])
 
         def g_copy(r, j, engine):
             if r not in grouped:
@@ -164,12 +167,15 @@ def tile_denseshift_t_kernel(tc, x, shift, sign, bias, grad_out, out):
                 accs[(r, j)] = acc
 
         def g_store(r):
-            result = outs.tile([P, J * IN_DIM], F32, name="result", tag="result")
+            m = r // 2
+            if m not in results:
+                results[m] = outs.tile([P, GJ * IN_DIM], F32, name="result", tag="result")
             for j in range(J):
-                copy_on("v" if j == J - 1 else "s", result[:, j * IN_DIM : (j + 1) * IN_DIM], accs[(r, j)][:])
-            dst = out[r * J * P : (r + 1) * J * P, :].rearrange("(p j) n -> p j n", j=J)
-            src = result[:].rearrange("p (j n) -> p j n", j=J)
-            for j0, nj in STORE_PIECES.get(r, ((0, J),)):
+                jj = (r % 2) * J + j
+                copy_on("v" if j == J - 1 else "s", results[m][:, jj * IN_DIM : (jj + 1) * IN_DIM], accs[(r, j)][:])
+            dst = out[m * GJ * P : (m + 1) * GJ * P, :].rearrange("(p j) n -> p j n", j=GJ)
+            src = results[m][:].rearrange("p (j n) -> p j n", j=GJ)
+            for j0, nj in STORE_PIECES.get(r, ()):
                 nc.sync.dma_start(out=dst[:, j0 : j0 + nj, :], in_=src[:, j0 : j0 + nj, :])
 
         def g_prepare(r):

@@ -20,11 +20,9 @@ WORDS = OUT_DIM // 2
 W_TILES = IN_DIM // P
 J = 4
 ROUNDS = TOKENS // (J * P)
-GJ = 2 * J
-GROUPS = ROUNDS // 2
 LN2 = math.log(2.0)
-LOAD_PIECES = {0: ((0, 1), (1, 1), (2, 2), (4, 2), (6, 2)), 1: ((0, 4), (4, 4))}
-STORE_PIECES = {1: ((0, 8),), 3: ((0, 8),), 4: ((0, 4),), 5: ((4, 2), (6, 2)), 6: ((0, 1), (1, 1), (2, 1), (3, 1)), 7: ((4, 1), (5, 1), (6, 1), (7, 1))}
+LOAD_PIECES = {0: ((0, 1), (1, 1), (2, 2)), 1: ((0, 2), (2, 2))}
+STORE_PIECES = {4: ((0, 2), (2, 2)), 5: ((0, 2), (2, 2)), 6: ((0, 2), (2, 2)), 7: ((0, 2), (2, 1), (3, 1))}
 DUMMIES = 0
 
 FLOPS = 2 * TOKENS * IN_DIM * OUT_DIM
@@ -36,8 +34,8 @@ def tile_denseshift_t_kernel(tc, x, shift, sign, bias, grad_out, out):
 
     with ExitStack() as ctx:
         keep = ctx.enter_context(tc.tile_pool(name="keep", bufs=1))
-        ring = ctx.enter_context(tc.tile_pool(name="ring", bufs=3))
-        outs = ctx.enter_context(tc.tile_pool(name="outs", bufs=4))
+        ring = ctx.enter_context(tc.tile_pool(name="ring", bufs=4))
+        outs = ctx.enter_context(tc.tile_pool(name="outs", bufs=6))
         psum = ctx.enter_context(tc.psum_pool(name="psum", bufs=1))
         ctx.enter_context(tc.manual_schedule())
 
@@ -55,11 +53,11 @@ def tile_denseshift_t_kernel(tc, x, shift, sign, bias, grad_out, out):
             nc.sync.dma_start(out=shift_sb[:, cols], in_=shift[rows, :])
             nc.sync.dma_start(out=sign_sb[:, cols], in_=sign[rows, :])
         g_raw = []
-        for m in range(GROUPS):
-            g_tile = keep.tile([P, GJ * OUT_DIM], BF16, name="g_raw%d" % m)
-            src = grad_out[m * GJ * P : (m + 1) * GJ * P, :].rearrange("(p j) k -> p j k", j=GJ)
-            dst = g_tile[:].rearrange("p (j k) -> p j k", j=GJ)
-            for j0, nj in LOAD_PIECES.get(m, ((0, GJ),)):
+        for r in range(ROUNDS):
+            g_tile = keep.tile([P, J * OUT_DIM], BF16, name="g_raw%d" % r)
+            src = grad_out[r * J * P : (r + 1) * J * P, :].rearrange("(p j) k -> p j k", j=J)
+            dst = g_tile[:].rearrange("p (j k) -> p j k", j=J)
+            for j0, nj in LOAD_PIECES.get(r, ((0, J),)):
                 nc.sync.dma_start(out=dst[:, j0 : j0 + nj, :], in_=src[:, j0 : j0 + nj, :])
             g_raw.append(g_tile)
 
@@ -130,10 +128,9 @@ def tile_denseshift_t_kernel(tc, x, shift, sign, bias, grad_out, out):
         results = {}
 
         def g_transpose(r, j0, nj):
-            words = g_raw[r // 2][:].bitcast(F32)
+            words = g_raw[r][:].bitcast(F32)
             for j in range(j0, j0 + nj):
-                jj = (r % 2) * J + j
-                banks[(r, j)] = transpose_row_tile(words[:, jj * WORDS : (jj + 1) * WORDS])
+                banks[(r, j)] = transpose_row_tile(words[:, j * WORDS : (j + 1) * WORDS])
 
         def g_copy(r, j, engine):
             if r not in grouped:
@@ -167,23 +164,28 @@ def tile_denseshift_t_kernel(tc, x, shift, sign, bias, grad_out, out):
                 accs[(r, j)] = acc
 
         def g_store(r):
-            m = r // 2
-            if m not in results:
-                results[m] = outs.tile([P, GJ * IN_DIM], F32, name="result", tag="result")
+            result = outs.tile([P, J * IN_DIM], F32, name="result", tag="result")
             for j in range(J):
-                jj = (r % 2) * J + j
-                copy_on("v" if j == J - 1 else "s", results[m][:, jj * IN_DIM : (jj + 1) * IN_DIM], accs[(r, j)][:])
-            dst = out[m * GJ * P : (m + 1) * GJ * P, :].rearrange("(p j) n -> p j n", j=GJ)
-            src = results[m][:].rearrange("p (j n) -> p j n", j=GJ)
-            for j0, nj in STORE_PIECES.get(r, ()):
+                copy_on("v" if j == J - 1 else "s", result[:, j * IN_DIM : (j + 1) * IN_DIM], accs[(r, j)][:])
+            dst = out[r * J * P : (r + 1) * J * P, :].rearrange("(p j) n -> p j n", j=J)
+            src = result[:].rearrange("p (j n) -> p j n", j=J)
+            for j0, nj in STORE_PIECES.get(r, ((0, J),)):
                 nc.sync.dma_start(out=dst[:, j0 : j0 + nj, :], in_=src[:, j0 : j0 + nj, :])
 
-        def g_prepare(r):
-            g_transpose(r, 0, J)
-            for j in range(J):
-                g_copy(r, j, "sv"[j % 2])
-            g_quantise(r, 0, 2)
-            g_quantise(r, 2, 2)
+        def g_prepare(run):
+            for r in run:
+                g_transpose(r, 0, J)
+            for r in run:
+                for j in range(J):
+                    g_copy(r, j, "sv"[j % 2])
+                g_quantise(r, 0, 2)
+                g_quantise(r, 2, 2)
+
+        def g_finish(run):
+            for r in run:
+                g_multiply(r)
+            for r in run:
+                g_store(r)
 
         w_exp(0)
         w_plus_minus(0)
@@ -217,8 +219,14 @@ def tile_denseshift_t_kernel(tc, x, shift, sign, bias, grad_out, out):
         g_copy(0, 2, "s")
         g_copy(0, 3, "v")
         g_quantise(0, 2, 2)
-        for r in range(ROUNDS):
-            if r + 1 < ROUNDS:
-                g_prepare(r + 1)
-            g_multiply(r)
-            g_store(r)
+        g_prepare((1,))
+        g_finish((0,))
+        g_prepare((2, 3))
+        g_finish((1,))
+        g_prepare((4, 5))
+        g_finish((2, 3))
+        g_prepare((6,))
+        g_finish((4, 5))
+        g_prepare((7,))
+        g_finish((6,))
+        g_finish((7,))

@@ -19,11 +19,12 @@ PASSES = OUT_DIM // 512
 WORDS = OUT_DIM // 2
 W_TILES = IN_DIM // P
 J = 4
-ROUNDS = TOKENS // (J * P)
+B = 8
+BLOCKS = TOKENS // (B * P)
 LN2 = math.log(2.0)
-LOAD_PIECES = {0: ((0, 1), (1, 1), (2, 2)), 1: ((0, 2), (2, 2))}
-STORE_PIECES = {4: ((0, 2), (2, 2)), 5: ((0, 2), (2, 2)), 6: ((0, 2), (2, 2)), 7: ((0, 2), (2, 1), (3, 1))}
-DUMMIES = 0
+LOAD_PIECES = {0: ((0, 1), (1, 1), (2, 2), (4, 2), (6, 2)), 1: ((0, 4), (4, 4)), 2: ((0, 4), (4, 4)), 3: ((0, 8),)}
+STORE_PIECES = {0: ((0, 8),), 1: ((0, 4), (4, 4)), 2: ((0, 4), (4, 4)), 3: ((0, 2), (2, 2), (4, 2), (6, 2))}
+LAG = 3
 
 FLOPS = 2 * TOKENS * IN_DIM * OUT_DIM
 BYTES = 2 * IN_DIM * OUT_DIM * 2 + TOKENS * OUT_DIM * 2 + TOKENS * IN_DIM * 4
@@ -35,7 +36,6 @@ def tile_denseshift_t_kernel(tc, x, shift, sign, bias, grad_out, out):
     with ExitStack() as ctx:
         keep = ctx.enter_context(tc.tile_pool(name="keep", bufs=1))
         ring = ctx.enter_context(tc.tile_pool(name="ring", bufs=4))
-        outs = ctx.enter_context(tc.tile_pool(name="outs", bufs=6))
         psum = ctx.enter_context(tc.psum_pool(name="psum", bufs=1))
         ctx.enter_context(tc.manual_schedule())
 
@@ -53,11 +53,11 @@ def tile_denseshift_t_kernel(tc, x, shift, sign, bias, grad_out, out):
             nc.sync.dma_start(out=shift_sb[:, cols], in_=shift[rows, :])
             nc.sync.dma_start(out=sign_sb[:, cols], in_=sign[rows, :])
         g_raw = []
-        for r in range(ROUNDS):
-            g_tile = keep.tile([P, J * OUT_DIM], BF16, name="g_raw%d" % r)
-            src = grad_out[r * J * P : (r + 1) * J * P, :].rearrange("(p j) k -> p j k", j=J)
-            dst = g_tile[:].rearrange("p (j k) -> p j k", j=J)
-            for j0, nj in LOAD_PIECES.get(r, ((0, J),)):
+        for b in range(BLOCKS):
+            g_tile = keep.tile([P, B * OUT_DIM], BF16, name="g_raw%d" % b)
+            src = grad_out[b * B * P : (b + 1) * B * P, :].rearrange("(p j) k -> p j k", j=B)
+            dst = g_tile[:].rearrange("p (j k) -> p j k", j=B)
+            for j0, nj in LOAD_PIECES[b]:
                 nc.sync.dma_start(out=dst[:, j0 : j0 + nj, :], in_=src[:, j0 : j0 + nj, :])
             g_raw.append(g_tile)
 
@@ -83,7 +83,6 @@ def tile_denseshift_t_kernel(tc, x, shift, sign, bias, grad_out, out):
             return bank[:].rearrange("p (g u r) -> p g r u", g=PASSES, u=2)
 
         pow2 = keep.tile([P, W_TILES * OUT_DIM], BF16, name="pow2")
-        plus_minus = keep.tile([P, W_TILES * OUT_DIM], BF16, name="plus_minus")
         w_sb = keep.tile([P, W_TILES * OUT_DIM], BF16, name="w_sb")
         w_grouped = keep.tile([P, PASSES * IN_DIM * 4], BF16, name="w_grouped", align_bytes=64)
         w_codes = keep.tile([P, PASSES * IN_DIM], U32, name="w_codes", align_bytes=64)
@@ -97,12 +96,12 @@ def tile_denseshift_t_kernel(tc, x, shift, sign, bias, grad_out, out):
         def w_plus_minus(j):
             cols = slice(j * OUT_DIM, (j + 1) * OUT_DIM)
             nc.vector.tensor_scalar(
-                out=plus_minus[:, cols], in0=sign_sb[:, cols], scalar1=-2.0, scalar2=1.0, op0=ALU.mult, op1=ALU.add
+                out=sign_sb[:, cols], in0=sign_sb[:, cols], scalar1=-2.0, scalar2=1.0, op0=ALU.mult, op1=ALU.add
             )
 
         def w_mult(j):
             cols = slice(j * OUT_DIM, (j + 1) * OUT_DIM)
-            nc.vector.tensor_tensor(out=w_sb[:, cols], in0=pow2[:, cols], in1=plus_minus[:, cols], op=ALU.mult)
+            nc.vector.tensor_tensor(out=w_sb[:, cols], in0=pow2[:, cols], in1=sign_sb[:, cols], op=ALU.mult)
 
         def w_transpose(j):
             w_banks[j] = transpose_row_tile(w_sb[:].bitcast(F32)[:, j * WORDS : (j + 1) * WORDS])
@@ -127,65 +126,95 @@ def tile_denseshift_t_kernel(tc, x, shift, sign, bias, grad_out, out):
         accs = {}
         results = {}
 
-        def g_transpose(r, j0, nj):
-            words = g_raw[r][:].bitcast(F32)
-            for j in range(j0, j0 + nj):
-                banks[(r, j)] = transpose_row_tile(words[:, j * WORDS : (j + 1) * WORDS])
+        def transpose(t):
+            words = g_raw[t // B][:].bitcast(F32)
+            banks[t] = transpose_row_tile(words[:, (t % B) * WORDS : (t % B + 1) * WORDS])
 
-        def g_copy(r, j, engine):
+        def copy_in(t, engine):
+            r, j = divmod(t, J)
             if r not in grouped:
                 grouped[r] = ring.tile([P, J * OUT_DIM], BF16, name="grouped", tag="grouped", align_bytes=64)
                 codes[r] = ring.tile([P, J * OUT_DIM // 4], U32, name="codes", tag="codes", align_bytes=64)
                 scales[r] = ring.tile([P, J * OUT_DIM // 4], U8, name="scales", tag="scales", align_bytes=64)
             dst = grouped[r][:].bitcast(F32)[:, j * WORDS : (j + 1) * WORDS]
-            copy_on(engine, dst.rearrange("p (g r u) -> p g r u", g=PASSES, u=2), pairs_side_by_side(banks[(r, j)]))
+            copy_on(engine, dst.rearrange("p (g r u) -> p g r u", g=PASSES, u=2), pairs_side_by_side(banks[t]))
 
-        def g_quantise(r, j0, nj):
+        def quantise(t, n):
+            r, j0 = divmod(t, J)
             nc.vector.quantize_mx(
-                out=codes[r][:, j0 * 256 : (j0 + nj) * 256].bitcast(E5M2X4),
-                scales=scales[r][:, j0 * 256 : (j0 + nj) * 256],
-                in_=grouped[r][:, j0 * OUT_DIM : (j0 + nj) * OUT_DIM],
+                out=codes[r][:, j0 * 256 : (j0 + n) * 256].bitcast(E5M2X4),
+                scales=scales[r][:, j0 * 256 : (j0 + n) * 256],
+                in_=grouped[r][:, j0 * OUT_DIM : (j0 + n) * OUT_DIM],
             )
 
-        def g_multiply(r):
-            for j in range(J):
-                acc = next_bank()
-                for g in range(PASSES):
-                    words = slice((j * PASSES + g) * P, (j * PASSES + g + 1) * P)
-                    nc.tensor.matmul_mx(
-                        out=acc[:],
-                        lhsT=codes[r][:, words].bitcast(E5M2X4),
-                        lhsT_scale=scales[r][:, words],
-                        rhs=w_codes[:, g * IN_DIM : (g + 1) * IN_DIM].bitcast(E4M3X4),
-                        rhs_scale=w_scales[:, g * IN_DIM : (g + 1) * IN_DIM],
-                        start=(g == 0),
-                        stop=(g == PASSES - 1),
-                    )
-                accs[(r, j)] = acc
+        def multiply(t):
+            r, j = divmod(t, J)
+            acc = next_bank()
+            for g in range(PASSES):
+                words = slice((j * PASSES + g) * P, (j * PASSES + g + 1) * P)
+                nc.tensor.matmul_mx(
+                    out=acc[:],
+                    lhsT=codes[r][:, words].bitcast(E5M2X4),
+                    lhsT_scale=scales[r][:, words],
+                    rhs=w_codes[:, g * IN_DIM : (g + 1) * IN_DIM].bitcast(E4M3X4),
+                    rhs_scale=w_scales[:, g * IN_DIM : (g + 1) * IN_DIM],
+                    start=(g == 0),
+                    stop=(g == PASSES - 1),
+                )
+            accs[t] = acc
 
-        def g_store(r):
-            result = outs.tile([P, J * IN_DIM], F32, name="result", tag="result")
-            for j in range(J):
-                copy_on("v" if j == J - 1 else "s", result[:, j * IN_DIM : (j + 1) * IN_DIM], accs[(r, j)][:])
-            dst = out[r * J * P : (r + 1) * J * P, :].rearrange("(p j) n -> p j n", j=J)
-            src = result[:].rearrange("p (j n) -> p j n", j=J)
-            for j0, nj in STORE_PIECES.get(r, ((0, J),)):
-                nc.sync.dma_start(out=dst[:, j0 : j0 + nj, :], in_=src[:, j0 : j0 + nj, :])
+        def copy_out(t, engine):
+            b, j = divmod(t, B)
+            if b not in results:
+                results[b] = keep.tile([P, B * IN_DIM], F32, name="result%d" % b)
+            copy_on(engine, results[b][:, j * IN_DIM : (j + 1) * IN_DIM], accs[t][:])
+            for j0, nj in STORE_PIECES[b]:
+                if j0 + nj - 1 == j:
+                    dst = out[b * B * P : (b + 1) * B * P, :].rearrange("(p j) n -> p j n", j=B)
+                    src = results[b][:].rearrange("p (j n) -> p j n", j=B)
+                    nc.sync.dma_start(out=dst[:, j0 : j0 + nj, :], in_=src[:, j0 : j0 + nj, :])
 
-        def g_prepare(run):
-            for r in run:
-                g_transpose(r, 0, J)
-            for r in run:
-                for j in range(J):
-                    g_copy(r, j, "sv"[j % 2])
-                g_quantise(r, 0, 2)
-                g_quantise(r, 2, 2)
+        def t_run(first, n, early=0):
+            for i in range(n + LAG):
+                if i < n:
+                    transpose(first + i)
+                if i >= LAG:
+                    c = first + i - LAG
+                    copy_in(c, "sv"[c % 2])
+                    if c % 2 == 1 and c - first < early:
+                        quantise(c - 1, 2)
 
-        def g_finish(run):
-            for r in run:
-                g_multiply(r)
-            for r in run:
-                g_store(r)
+        def m_run(first, n, q_first, q_n, engines):
+            for t in range(q_first, q_first + q_n, 2):
+                quantise(t, 2)
+            for i in range(n + 1):
+                if i < n:
+                    multiply(first + i)
+                if i >= 1:
+                    copy_out(first + i - 1, engines[(first + i - 1) % len(engines)])
+
+        def prepare(rounds, quantised=99):
+            tiles = [r * J + j for r in rounds for j in range(J)]
+            for i in range(len(tiles) + 8):
+                if i >= 8:
+                    c = tiles[i - 8]
+                    copy_in(c, "sv"[c % 2])
+                    if c % J == J - 1 and (i - 8) // J < quantised:
+                        quantise(c - 3, 2)
+                        quantise(c - 1, 2)
+                if i < len(tiles):
+                    transpose(tiles[i])
+
+        def finish(rounds, late=()):
+            tiles = [r * J + j for r in rounds for j in range(J)]
+            for r in late:
+                quantise(r * J, 2)
+                quantise(r * J + 2, 2)
+            for i in range(len(tiles) + 4):
+                if i >= 4:
+                    copy_out(tiles[i - 4], "sssv"[tiles[i - 4] % J])
+                if i < len(tiles):
+                    multiply(tiles[i])
 
         w_exp(0)
         w_plus_minus(0)
@@ -201,32 +230,33 @@ def tile_denseshift_t_kernel(tc, x, shift, sign, bias, grad_out, out):
         w_transpose(2)
         w_exp(3)
         w_plus_minus(3)
-        g_transpose(0, 0, 1)
+        transpose(0)
         w_mult(3)
         w_transpose(3)
         w_copy(0, "s")
         w_quantise(0)
-        g_copy(0, 0, "v")
+        copy_in(0, "v")
         w_copy(1, "s")
         w_quantise(1)
-        g_transpose(0, 1, 3)
+        transpose(1)
+        transpose(2)
+        transpose(3)
         w_copy(2, "s")
         w_quantise(2)
-        g_copy(0, 1, "v")
-        g_quantise(0, 0, 2)
+        copy_in(1, "v")
+        quantise(0, 2)
         w_copy(3, "s")
         w_quantise(3)
-        g_copy(0, 2, "s")
-        g_copy(0, 3, "v")
-        g_quantise(0, 2, 2)
-        g_prepare((1,))
-        g_finish((0,))
-        g_prepare((2, 3))
-        g_finish((1,))
-        g_prepare((4, 5))
-        g_finish((2, 3))
-        g_prepare((6,))
-        g_finish((4, 5))
-        g_prepare((7,))
-        g_finish((6,))
-        g_finish((7,))
+        copy_in(2, "s")
+        copy_in(3, "v")
+        quantise(2, 2)
+        prepare((1,))
+        finish((0,))
+        prepare((2, 3))
+        finish((1,))
+        prepare((4, 5))
+        finish((2, 3))
+        prepare((6,))
+        finish((4, 5))
+        prepare((7,))
+        finish((6, 7))

@@ -23,7 +23,7 @@ B = 8
 BLOCKS = TOKENS // (B * P)
 LN2 = math.log(2.0)
 LOAD_PIECES = {0: ((0, 1), (1, 1), (2, 2), (4, 2), (6, 2)), 1: ((0, 4), (4, 4)), 2: ((0, 4), (4, 4)), 3: ((0, 8),)}
-STORE_PIECES = {0: ((0, 8),), 1: ((0, 4), (4, 4)), 2: ((0, 4), (4, 4)), 3: ((0, 2), (2, 2), (4, 2), (6, 2))}
+STORE_PIECES = {0: ((0, 8),), 1: ((0, 4), (4, 4)), 2: ((0, 2), (2, 2), (4, 4)), 3: ((0, 2), (2, 2), (4, 2), (6, 2))}
 LAG = 3
 
 FLOPS = 2 * TOKENS * IN_DIM * OUT_DIM
@@ -205,12 +205,13 @@ def tile_denseshift_t_kernel(tc, x, shift, sign, bias, grad_out, out):
                 if i < len(tiles):
                     transpose(tiles[i])
 
-        def finish(rounds, late=()):
+        def finish(rounds, late=(), after=0):
             tiles = [r * J + j for r in rounds for j in range(J)]
-            for r in late:
-                quantise(r * J, 2)
-                quantise(r * J + 2, 2)
             for i in range(len(tiles) + 4):
+                if i == 4 + after * J:
+                    for r in late:
+                        quantise(r * J, 2)
+                        quantise(r * J + 2, 2)
                 if i >= 4:
                     copy_out(tiles[i - 4], "sssv"[tiles[i - 4] % J])
                 if i < len(tiles):
@@ -253,10 +254,8 @@ def tile_denseshift_t_kernel(tc, x, shift, sign, bias, grad_out, out):
         prepare((1,))
         finish((0,))
         prepare((2, 3))
-        finish((1,))
-        prepare((4, 5))
-        finish((2, 3))
-        prepare((6,))
-        finish((4, 5))
+        finish((1, 2, 3))
+        prepare((4, 5, 6), 2)
+        finish((4, 5), (6,), 1)
         prepare((7,))
         finish((6, 7))

@@ -23,7 +23,7 @@ B = 8
 BLOCKS = TOKENS // (B * P)
 LN2 = math.log(2.0)
 LOAD_PIECES = {0: ((0, 1), (1, 1), (2, 2), (4, 2), (6, 2)), 1: ((0, 4), (4, 4)), 2: ((0, 4), (4, 4)), 3: ((0, 8),)}
-STORE_PIECES = {0: ((0, 8),), 1: ((0, 4), (4, 4)), 2: ((0, 2), (2, 2), (4, 4)), 3: ((0, 2), (2, 2), (4, 2), (6, 2))}
+STORE_PIECES = {0: ((0, 8),), 1: ((0, 4), (4, 4)), 2: ((0, 2), (2, 2), (4, 4)), 3: ((0, 2), (2, 2), (4, 2), (6, 1), (7, 1))}
 LAG = 3
 
 FLOPS = 2 * TOKENS * IN_DIM * OUT_DIM

@@ -23,7 +23,7 @@ B = 8
 BLOCKS = TOKENS // (B * P)
 LN2 = math.log(2.0)
 LOAD_PIECES = {0: ((0, 1), (1, 1), (2, 2), (4, 2), (6, 2)), 1: ((0, 4), (4, 4)), 2: ((0, 4), (4, 4)), 3: ((0, 8),)}
-STORE_PIECES = {0: ((0, 8),), 1: ((0, 4), (4, 4)), 2: ((0, 2), (2, 2), (4, 4)), 3: ((0, 2), (2, 2), (4, 2), (6, 1), (7, 1))}
+STORE_PIECES = {0: ((0, 8),), 1: ((0, 4), (4, 4)), 2: ((0, 2), (2, 2), (4, 4)), 3: ((0, 2), (2, 2), (4, 2), (6, 1))}
 LAG = 3
 
 FLOPS = 2 * TOKENS * IN_DIM * OUT_DIM
@@ -174,6 +174,15 @@ def tile_denseshift_t_kernel(tc, x, shift, sign, bias, grad_out, out):
                     src = results[b][:].rearrange("p (j n) -> p j n", j=B)
                     nc.sync.dma_start(out=dst[:, j0 : j0 + nj, :], in_=src[:, j0 : j0 + nj, :])
 
+        def copy_out_halves(t, engine):
+            b, j = divmod(t, B)
+            dst = out[b * B * P : (b + 1) * B * P, :].rearrange("(p j) n -> p j n", j=B)
+            src = results[b][:].rearrange("p (j n) -> p j n", j=B)
+            for h in range(2):
+                cols = slice(h * IN_DIM // 2, (h + 1) * IN_DIM // 2)
+                copy_on(engine, results[b][:, j * IN_DIM + h * IN_DIM // 2 : j * IN_DIM + (h + 1) * IN_DIM // 2], accs[t][:, cols])
+                nc.sync.dma_start(out=dst[:, j : j + 1, cols], in_=src[:, j : j + 1, cols])
+
         def t_run(first, n, early=0):
             for i in range(n + LAG):
                 if i < n:
@@ -212,7 +221,9 @@ def tile_denseshift_t_kernel(tc, x, shift, sign, bias, grad_out, out):
                     for r in late:
                         quantise(r * J, 2)
                         quantise(r * J + 2, 2)
-                if i >= 4:
+                if i >= 4 and tiles[i - 4] == TOKENS // P - 1:
+                    copy_out_halves(tiles[i - 4], "v")
+                elif i >= 4:
                     copy_out(tiles[i - 4], "sssv"[tiles[i - 4] % J])
                 if i < len(tiles):
                     multiply(tiles[i])

import math
from contextlib import ExitStack

import concourse.mybir as mybir
from concourse.masks import make_identity

F32 = mybir.dt.float32
BF16 = mybir.dt.bfloat16
U32 = mybir.dt.uint32
U8 = mybir.dt.uint8
E4M3X4 = mybir.dt.float8_e4m3fn_x4
E5M2X4 = mybir.dt.float8_e5m2_x4
ALU = mybir.AluOpType
ACT = mybir.ActivationFunctionType

P = 128
TOKENS, IN_DIM, OUT_DIM = 4096, 512, 1024
PASSES = OUT_DIM // 512
WORDS = OUT_DIM // 2
W_TILES = IN_DIM // P
J = 4
B = 8
BLOCKS = TOKENS // (B * P)
LN2 = math.log(2.0)
LOAD_PIECES = {0: ((0, 1), (1, 1), (2, 2), (4, 2), (6, 2)), 1: ((0, 4), (4, 4)), 2: ((0, 4), (4, 4)), 3: ((0, 8),)}
STORE_PIECES = {0: ((0, 8),), 1: ((0, 4), (4, 4)), 2: ((0, 2), (2, 2), (4, 4)), 3: ((0, 2), (2, 2), (4, 2), (6, 1))}
LAG = 3

FLOPS = 2 * TOKENS * IN_DIM * OUT_DIM
BYTES = 2 * IN_DIM * OUT_DIM * 2 + TOKENS * OUT_DIM * 2 + TOKENS * IN_DIM * 4


def tile_denseshift_t_kernel(tc, x, shift, sign, bias, grad_out, out):
    nc = tc.nc

    with ExitStack() as ctx:
        keep = ctx.enter_context(tc.tile_pool(name="keep", bufs=1))
        ring = ctx.enter_context(tc.tile_pool(name="ring", bufs=4))
        psum = ctx.enter_context(tc.psum_pool(name="psum", bufs=1))
        ctx.enter_context(tc.manual_schedule())

        ident = keep.tile([P, P], F32, name="ident")
        make_identity(nc, ident[:])
        tiny = keep.tile([P, 2], F32, name="tiny")
        nc.vector.memset(tiny[:, 0:1], 0.0)
        nc.scalar.activation(out=tiny[:, 1:2], in_=tiny[:, 0:1], func=ACT.Exp)

        shift_sb = keep.tile([P, W_TILES * OUT_DIM], BF16, name="shift_sb")
        sign_sb = keep.tile([P, W_TILES * OUT_DIM], BF16, name="sign_sb")
        for j in range(W_TILES):
            cols = slice(j * OUT_DIM, (j + 1) * OUT_DIM)
            rows = slice(j * P, (j + 1) * P)
            nc.sync.dma_start(out=shift_sb[:, cols], in_=shift[rows, :])
            nc.sync.dma_start(out=sign_sb[:, cols], in_=sign[rows, :])
        g_raw = []
        for b in range(BLOCKS):
            g_tile = keep.tile([P, B * OUT_DIM], BF16, name="g_raw%d" % b)
            src = grad_out[b * B * P : (b + 1) * B * P, :].rearrange("(p j) k -> p j k", j=B)
            dst = g_tile[:].rearrange("p (j k) -> p j k", j=B)
            for j0, nj in LOAD_PIECES[b]:
                nc.sync.dma_start(out=dst[:, j0 : j0 + nj, :], in_=src[:, j0 : j0 + nj, :])
            g_raw.append(g_tile)

        taken = []

        def next_bank():
            taken.append(1)
            return psum.tile([P, 512], F32, name="bank", tag="bank%d" % ((len(taken) - 1) % 8))

        def transpose_row_tile(words):
            bank = next_bank()
            for q in range(WORDS // P):
                nc.tensor.transpose(bank[:, q * P : (q + 1) * P], words[:, q * P : (q + 1) * P], ident[:])
            return bank

        def copy_on(engine, dst, src):
            if engine == "v":
                nc.vector.tensor_copy(out=dst, in_=src)
            else:
                nc.scalar.copy(out=dst, in_=src)

        def pairs_side_by_side(bank):
            return bank[:].rearrange("p (g u r) -> p g r u", g=PASSES, u=2)

        pow2 = keep.tile([P, W_TILES * OUT_DIM], BF16, name="pow2")
        w_sb = keep.tile([P, W_TILES * OUT_DIM], BF16, name="w_sb")
        w_grouped = keep.tile([P, PASSES * IN_DIM * 4], BF16, name="w_grouped", align_bytes=64)
        w_codes = keep.tile([P, PASSES * IN_DIM], U32, name="w_codes", align_bytes=64)
        w_scales = keep.tile([P, PASSES * IN_DIM], U8, name="w_scales", align_bytes=64)
        w_banks = {}

        def w_exp(j):
            cols = slice(j * OUT_DIM, (j + 1) * OUT_DIM)
            nc.scalar.activation(out=pow2[:, cols], in_=shift_sb[:, cols], func=ACT.Exp, scale=LN2)

        def w_plus_minus(j):
            cols = slice(j * OUT_DIM, (j + 1) * OUT_DIM)
            nc.vector.tensor_scalar(
                out=sign_sb[:, cols], in0=sign_sb[:, cols], scalar1=-2.0, scalar2=1.0, op0=ALU.mult, op1=ALU.add
            )

        def w_mult(j):
            cols = slice(j * OUT_DIM, (j + 1) * OUT_DIM)
            nc.vector.tensor_tensor(out=w_sb[:, cols], in0=pow2[:, cols], in1=sign_sb[:, cols], op=ALU.mult)

        def w_transpose(j):
            w_banks[j] = transpose_row_tile(w_sb[:].bitcast(F32)[:, j * WORDS : (j + 1) * WORDS])

        def w_copy(j, engine):
            dst = w_grouped[:].bitcast(F32).rearrange("p (g n u) -> p g n u", g=PASSES, u=2)
            copy_on(engine, dst[:, :, j * P : (j + 1) * P, :], pairs_side_by_side(w_banks[j]))

        def w_quantise(j):
            for g in range(PASSES):
                words = slice(g * IN_DIM + j * P, g * IN_DIM + (j + 1) * P)
                nc.vector.quantize_mx(
                    out=w_codes[:, words].bitcast(E4M3X4),
                    scales=w_scales[:, words],
                    in_=w_grouped[:, 4 * (g * IN_DIM + j * P) : 4 * (g * IN_DIM + (j + 1) * P)],
                )

        banks = {}
        grouped = {}
        codes = {}
        scales = {}
        accs = {}
        results = {}

        def transpose(t):
            words = g_raw[t // B][:].bitcast(F32)
            banks[t] = transpose_row_tile(words[:, (t % B) * WORDS : (t % B + 1) * WORDS])

        def copy_in(t, engine):
            r, j = divmod(t, J)
            if r not in grouped:
                grouped[r] = ring.tile([P, J * OUT_DIM], BF16, name="grouped", tag="grouped", align_bytes=64)
                codes[r] = ring.tile([P, J * OUT_DIM // 4], U32, name="codes", tag="codes", align_bytes=64)
                scales[r] = ring.tile([P, J * OUT_DIM // 4], U8, name="scales", tag="scales", align_bytes=64)
            dst = grouped[r][:].bitcast(F32)[:, j * WORDS : (j + 1) * WORDS]
            copy_on(engine, dst.rearrange("p (g r u) -> p g r u", g=PASSES, u=2), pairs_side_by_side(banks[t]))

        def quantise(t, n):
            r, j0 = divmod(t, J)
            nc.vector.quantize_mx(
                out=codes[r][:, j0 * 256 : (j0 + n) * 256].bitcast(E5M2X4),
                scales=scales[r][:, j0 * 256 : (j0 + n) * 256],
                in_=grouped[r][:, j0 * OUT_DIM : (j0 + n) * OUT_DIM],
            )

        def multiply(t):
            r, j = divmod(t, J)
            acc = next_bank()
            for g in range(PASSES):
                words = slice((j * PASSES + g) * P, (j * PASSES + g + 1) * P)
                nc.tensor.matmul_mx(
                    out=acc[:],
                    lhsT=codes[r][:, words].bitcast(E5M2X4),
                    lhsT_scale=scales[r][:, words],
                    rhs=w_codes[:, g * IN_DIM : (g + 1) * IN_DIM].bitcast(E4M3X4),
                    rhs_scale=w_scales[:, g * IN_DIM : (g + 1) * IN_DIM],
                    start=(g == 0),
                    stop=(g == PASSES - 1),
                )
            accs[t] = acc

        def copy_out(t, engine):
            b, j = divmod(t, B)
            if b not in results:
                results[b] = keep.tile([P, B * IN_DIM], F32, name="result%d" % b)
            copy_on(engine, results[b][:, j * IN_DIM : (j + 1) * IN_DIM], accs[t][:])
            for j0, nj in STORE_PIECES[b]:
                if j0 + nj - 1 == j:
                    dst = out[b * B * P : (b + 1) * B * P, :].rearrange("(p j) n -> p j n", j=B)
                    src = results[b][:].rearrange("p (j n) -> p j n", j=B)
                    nc.sync.dma_start(out=dst[:, j0 : j0 + nj, :], in_=src[:, j0 : j0 + nj, :])

        def copy_out_halves(t, engine):
            b, j = divmod(t, B)
            dst = out[b * B * P : (b + 1) * B * P, :].rearrange("(p j) n -> p j n", j=B)
            src = results[b][:].rearrange("p (j n) -> p j n", j=B)
            for h in range(2):
                cols = slice(h * IN_DIM // 2, (h + 1) * IN_DIM // 2)
                copy_on(engine, results[b][:, j * IN_DIM + h * IN_DIM // 2 : j * IN_DIM + (h + 1) * IN_DIM // 2], accs[t][:, cols])
                nc.sync.dma_start(out=dst[:, j : j + 1, cols], in_=src[:, j : j + 1, cols])

        def t_run(first, n, early=0):
            for i in range(n + LAG):
                if i < n:
                    transpose(first + i)
                if i >= LAG:
                    c = first + i - LAG
                    copy_in(c, "sv"[c % 2])
                    if c % 2 == 1 and c - first < early:
                        quantise(c - 1, 2)

        def m_run(first, n, q_first, q_n, engines):
            for t in range(q_first, q_first + q_n, 2):
                quantise(t, 2)
            for i in range(n + 1):
                if i < n:
                    multiply(first + i)
                if i >= 1:
                    copy_out(first + i - 1, engines[(first + i - 1) % len(engines)])

        def prepare(rounds, quantised=99):
            tiles = [r * J + j for r in rounds for j in range(J)]
            for i in range(len(tiles) + 8):
                if i >= 8:
                    c = tiles[i - 8]
                    copy_in(c, "sv"[c % 2])
                    if c % J == J - 1 and (i - 8) // J < quantised:
                        quantise(c - 3, 2)
                        quantise(c - 1, 2)
                if i < len(tiles):
                    transpose(tiles[i])

        def finish(rounds, late=(), after=0):
            tiles = [r * J + j for r in rounds for j in range(J)]
            for i in range(len(tiles) + 4):
                if i == 4 + after * J:
                    for r in late:
                        quantise(r * J, 2)
                        quantise(r * J + 2, 2)
                if i >= 4 and tiles[i - 4] == TOKENS // P - 1:
                    copy_out_halves(tiles[i - 4], "v")
                elif i >= 4:
                    copy_out(tiles[i - 4], "sssv"[tiles[i - 4] % J])
                if i < len(tiles):
                    multiply(tiles[i])

        w_exp(0)
        w_plus_minus(0)
        w_mult(0)
        w_transpose(0)
        w_exp(1)
        w_plus_minus(1)
        w_mult(1)
        w_transpose(1)
        w_exp(2)
        w_plus_minus(2)
        w_mult(2)
        w_transpose(2)
        w_exp(3)
        w_plus_minus(3)
        transpose(0)
        w_mult(3)
        w_transpose(3)
        w_copy(0, "s")
        w_quantise(0)
        copy_in(0, "v")
        w_copy(1, "s")
        w_quantise(1)
        transpose(1)
        transpose(2)
        transpose(3)
        w_copy(2, "s")
        w_quantise(2)
        copy_in(1, "v")
        quantise(0, 2)
        w_copy(3, "s")
        w_quantise(3)
        copy_in(2, "s")
        copy_in(3, "v")
        quantise(2, 2)
        prepare((1,))
        finish((0,))
        prepare((2, 3))
        finish((1, 2, 3))
        prepare((4, 5, 6), 2)
        finish((4, 5), (6,), 1)
        prepare((7,))
        finish((6, 7))
